import numpy as np
import ml_dtypes


def mxq(x, axis, fmt="e4m3"):
    dtype, down = {"e4m3": (ml_dtypes.float8_e4m3fn, 7), "e5m2": (ml_dtypes.float8_e5m2, 14)}[fmt]
    v = np.moveaxis(np.asarray(x, np.float32).astype(ml_dtypes.bfloat16).astype(np.float64), axis, -1)
    blocks = v.reshape(v.shape[:-1] + (-1, 32))
    amax = np.abs(blocks).max(-1, keepdims=True)
    byte = np.maximum(np.where(amax > 0, np.frexp(amax)[1] - 1 + 127, 0) - down, 1)
    scale = np.exp2(byte - 127.0)
    codes = (blocks / scale).astype(np.float32).astype(dtype).astype(np.float64)
    return np.moveaxis((codes * scale).reshape(v.shape), -1, axis)


WIDE = False


def mx_kscale(k):
    if not WIDE:
        return np.ones(k)
    levels = np.array([10, -10, 5, -5, 0])
    if k % 512:
        return np.exp2(np.random.permutation(np.resize(levels, k // 32))).repeat(32)
    a = np.empty((k // 512, 16))
    for p in range(k // 512):
        a[p, :8] = np.random.permutation(np.resize(levels, 8))
        for g in range(8):
            far = levels[np.abs(levels - a[p, g]) >= 10]
            a[p, g + 8] = far[np.random.randint(len(far))]
    return np.exp2(a.ravel()).repeat(32)


BF16 = ml_dtypes.bfloat16


def bf(x):
    return np.asarray(x, np.float32).astype(BF16)


def f64(x):
    return np.asarray(x).astype(np.float64)


S, B, H, NH, NG, HD, ROT = 512, 2, 1536, 12, 2, 128, 64
QW = NH * HD
KW = NG * HD
O = QW + KW + KW
HALF = ROT // 2


def apply_rope(x, rope):
    s = x.shape[0]
    half = rope.shape[-2]
    rot = half + half
    xr, xp = x[..., :rot], x[..., rot:]
    xs = xr.reshape(xr.shape[:-1] + (half, 2))
    rc = rope[:s].reshape(s, 1, 1, half, 2)
    c, sn = rc[..., 0], rc[..., 1]
    x0, x1 = xs[..., 0], xs[..., 1]
    out = np.stack([x0 * c - x1 * sn, x1 * c + x0 * sn], axis=-1)
    return np.concatenate([out.reshape(xr.shape), xp], axis=-1)


def draw0():
    s = mx_kscale(H)
    pos = np.arange(S, dtype=np.float64)
    inv_freq = 1.0 / (10000.0 ** (np.arange(0, HALF, dtype=np.float64) / HALF))
    ang = pos[:, None] * inv_freq[None, :]
    rope = np.stack([np.cos(ang), np.sin(ang)], axis=-1)[:, None]
    return {"hidden_states": bf(np.random.standard_normal((S, B, H)) * s),
            "rotary_pos_emb": bf(rope),
            "W_qkv": bf(np.random.standard_normal((O, H)) * 1.5 / np.sqrt(H) / s[None, :]),
            "b_qkv": bf(np.random.standard_normal(O) * 0.3)}


def core(hidden_states, rotary_pos_emb, W_qkv, b_qkv):
    x = f64(hidden_states)
    s, b = x.shape[0], x.shape[1]
    mixed = (mxq(x, 2, "e4m3") @ mxq(f64(W_qkv), 1, "e4m3").T) + f64(b_qkv)
    q = mixed[..., :QW].reshape(s, b, NH, HD)
    k = mixed[..., QW:QW + KW].reshape(s, b, NG, HD)
    v = mixed[..., QW + KW:].reshape(s, b, NG, HD)
    rope = f64(rotary_pos_emb)
    return apply_rope(q, rope), apply_rope(k, rope), v


def e4m3fn_bytes(y):
    return np.clip(np.asarray(y, np.float64), -448.0, 448.0).astype(np.float32).astype(ml_dtypes.float8_e4m3fn).view(np.uint8)


def e4m3fn_values(b):
    return np.asarray(b, np.uint8).view(ml_dtypes.float8_e4m3fn).astype(np.float64)


def setup_inputs():
    d = draw0()
    x0 = np.asarray(d['W_qkv']).astype(np.float64)
    s = (np.max(np.abs(x0), axis=(0,), keepdims=True) / 448.0).astype(np.float32)
    out = {}
    for k, v in d.items():
        if k == 'W_qkv':
            out['W_qkv_bytes'] = e4m3fn_bytes(x0 / s.astype(np.float64))
            out['W_qkv_scale'] = s
        else:
            out[k] = v
    return out


def reference(hidden_states, rotary_pos_emb, W_qkv_bytes, W_qkv_scale, b_qkv):
    return core(hidden_states, rotary_pos_emb, e4m3fn_values(W_qkv_bytes) * W_qkv_scale.astype(np.float64), b_qkv)

@@ -1,0 +1,275 @@
+from contextlib import ExitStack
+
+import concourse.mybir as mybir
+from concourse.masks import make_identity
+
+FLOPS = 2 * 1024 * 2048 * 1536
+
+F32 = mybir.dt.float32
+BF16 = mybir.dt.bfloat16
+U32 = mybir.dt.uint32
+U8 = mybir.dt.uint8
+FP8 = mybir.dt.float8_e4m3fn
+FP8X4 = mybir.dt.float8_e4m3fn_x4
+ALU = mybir.AluOpType
+ACT = mybir.ActivationFunctionType
+
+P = 128
+K = 1536
+PASSES = 3
+KW = K // 2
+ORDER = [3, 0, 1, 2]
+
+
+def tile_selfattention_pa_kernel(tc, hidden_states, rotary_pos_emb, W_qkv_bytes, W_qkv_scale, b_qkv, out_0, out_1, out_2):
+    nc = tc.nc
+    with ExitStack() as ctx:
+        const = ctx.enter_context(tc.tile_pool(name="const", bufs=1))
+        rawp = ctx.enter_context(tc.tile_pool(name="rawp", bufs=6))
+        wbytes = ctx.enter_context(tc.tile_pool(name="wbytes", bufs=8))
+        grpp = ctx.enter_context(tc.tile_pool(name="grpp", bufs=3))
+        msrp = ctx.enter_context(tc.tile_pool(name="msrp", bufs=4))
+        mspp = ctx.enter_context(tc.tile_pool(name="mspp", bufs=4))
+        pqp = ctx.enter_context(tc.tile_pool(name="pqp", bufs=3))
+        otp = ctx.enter_context(tc.tile_pool(name="otp", bufs=6))
+        prep_ps = ctx.enter_context(tc.psum_pool(name="prep_ps", bufs=2))
+        acc_ps = ctx.enter_context(tc.psum_pool(name="acc_ps", bufs=3))
+        back_ps = ctx.enter_context(tc.psum_pool(name="back_ps", bufs=3))
+        ctx.enter_context(tc.manual_schedule(engines={mybir.EngineType.PE}))
+
+        sc = const.tile([P, K], F32, tag="sc")
+        nc.scalar.dma_start(out=sc[:], in_=W_qkv_scale.rearrange("o k -> (o k)").partition_broadcast(P))
+        wb = {}
+        xraw = []
+
+        def load_w(jj, j2):
+            wb_t = wbytes.tile([P, 2, K], U8, tag="wb")
+            wb[(jj, j2)] = wb_t
+            r0 = jj * 512 + j2 * 256
+            nc.sync.dma_start(out=wb_t[:], in_=W_qkv_bytes[r0:r0 + 256, :].rearrange("(c p) k -> p c k", p=P))
+
+        def load_x(k):
+            xraw_t = rawp.tile([P, 2, K], BF16, tag="raw")
+            xraw.append(xraw_t)
+            nc.sync.dma_start(out=xraw_t[:], in_=hidden_states[k * P:(k + 1) * P, :, :])
+
+        load_w(ORDER[0], 0)
+        load_x(0)
+        load_w(ORDER[0], 1)
+        load_x(1)
+        load_x(2)
+        load_x(3)
+        for jj in ORDER[1:]:
+            load_w(jj, 0)
+            load_w(jj, 1)
+
+        rp = const.tile([P, 4, 64], BF16, tag="rp")
+        nc.scalar.dma_start(out=rp[:], in_=rotary_pos_emb.rearrange("(k p) o i e -> p k (o i e)", p=P))
+        brow = const.tile([P, P], BF16, tag="brow")
+        nc.gpsimd.memset(brow[:], 0.0)
+        bview = b_qkv.rearrange("(j a x f) -> x j a f", j=8, a=2, x=2, f=64)
+        for x in range(2):
+            nc.scalar.dma_start(out=brow[x * 8:(x + 1) * 8, :].rearrange("j (a f) -> j a f", a=2), in_=bview[x])
+
+        ident = const.tile([P, P], F32, tag="ident")
+        make_identity(nc, ident[:])
+        identb = const.tile([P, P], BF16, tag="identb")
+        make_identity(nc, identb[:])
+
+        tab = const.tile([P, 4, 2, 64], F32, tag="tab")
+        bfull = const.tile([P, 2048], BF16, tag="bfull")
+        nc.sync.dma_start(out=bfull[:], in_=b_qkv.partition_broadcast(P))
+        bias_col = const.tile([P, 16], F32, tag="bias_col")
+
+        def tables():
+            rpv = rp[:].rearrange("p k (i e) -> p k i e", e=2)
+            c2v = tab[:, :, 0, :].rearrange("p k (i e) -> p k i e", e=2)
+            snv = tab[:, :, 1, :].rearrange("p k (i e) -> p k i e", e=2)
+            nc.scalar.activation(out=c2v[:, :, :, 0], in_=rpv[:, :, :, 0], func=ACT.Copy, scale=1.0)
+            nc.scalar.activation(out=c2v[:, :, :, 1], in_=rpv[:, :, :, 0], func=ACT.Copy, scale=1.0)
+            nc.scalar.activation(out=snv[:, :, :, 0], in_=rpv[:, :, :, 1], func=ACT.Copy, scale=1.0)
+            nc.scalar.activation(out=snv[:, :, :, 1], in_=rpv[:, :, :, 1], func=ACT.Copy, scale=-1.0)
+
+        def bias_turn():
+            bt_ps = prep_ps.tile([P, P], BF16, tag="prep")
+            nc.tensor.transpose(bt_ps[:], brow[:], identb[:])
+            nc.scalar.copy(out=bias_col[:], in_=bt_ps[:, 0:16])
+
+        xcodes = const.tile([P, PASSES, 1024], U32, tag="xcodes", align_bytes=64)
+        xscales = const.tile([P, PASSES, 1024], U8, tag="xscales", align_bytes=64)
+        wcodes = const.tile([P, PASSES, 2048], U32, tag="wcodes", align_bytes=64)
+        wscales = const.tile([P, PASSES, 2048], U8, tag="wscales", align_bytes=64)
+
+        xg = {}
+        wg = {}
+        wbf = {}
+
+        def x_prep(k):
+            th, sb = k // 2, k % 2
+            if sb == 0:
+                xg_t = grpp.tile([P, PASSES, 2048], BF16, tag="grp", align_bytes=64)
+                xg[th] = xg_t
+            words = xraw[k][:].rearrange("p b k -> p (b k)").bitcast(F32)
+            xgw = xg[th][:].bitcast(F32)
+            for g in range(PASSES):
+                xt = prep_ps.tile([P, 2, 256], F32, tag="prep")
+                for b in range(2):
+                    for u in range(2):
+                        lo = b * KW + 256 * g
+                        nc.tensor.transpose(xt[:, u, b * P:(b + 1) * P], words[:, lo + u:lo + 256:2], ident[:])
+                nc.scalar.copy(out=xgw[:, g, sb * 512:(sb + 1) * 512].rearrange("p (r u) -> p r u", u=2),
+                               in_=xt[:].rearrange("p u r -> p r u"))
+
+        def x_quant(th):
+            for g in range(PASSES):
+                cols = slice(th * 512, (th + 1) * 512)
+                nc.vector.quantize_mx(out=xcodes[:, g, cols].bitcast(FP8X4), scales=xscales[:, g, cols], in_=xg[th][:, g, :])
+
+        def w_widen(jj, j2):
+            wbf_t = rawp.tile([P, 2, K], BF16, tag="raw")
+            wbf[(jj, j2)] = wbf_t
+            for a in range(2):
+                nc.vector.tensor_tensor(out=wbf_t[:, a, :], in0=wb[(jj, j2)][:, a, :].bitcast(FP8), in1=sc[:], op=ALU.mult)
+
+        def w_turn(jj, j2, gs):
+            if jj not in wg:
+                wg_t = grpp.tile([P, PASSES, 2048], BF16, tag="grp", align_bytes=64)
+                wg[jj] = wg_t
+            words = wbf[(jj, j2)][:].rearrange("p a k -> p (a k)").bitcast(F32)
+            wgw = wg[jj][:].bitcast(F32)
+            for g in gs:
+                wt = prep_ps.tile([P, 2, 256], F32, tag="prep")
+                for a in range(2):
+                    for u in range(2):
+                        lo = a * KW + 256 * g
+                        nc.tensor.transpose(wt[:, u, a * P:(a + 1) * P], words[:, lo + u:lo + 256:2], ident[:])
+                wtv = wt[:].rearrange("p u (a x f) -> p x a f u", a=2, x=2)
+                for x in range(2):
+                    lo = x * 512 + j2 * 256
+                    nc.scalar.copy(out=wgw[:, g, lo:lo + 256].rearrange("p (a f u) -> p a f u", a=2, u=2), in_=wtv[:, x])
+
+        def w_quant(jj, gs):
+            for g in gs:
+                cols = slice(jj * 512, (jj + 1) * 512)
+                nc.vector.quantize_mx(out=wcodes[:, g, cols].bitcast(FP8X4), scales=wscales[:, g, cols], in_=wg[jj][:, g, :])
+
+        ms = {}
+        ot = {}
+
+        def mx(jj, th, x):
+            tcols = slice(th * 512, (th + 1) * 512)
+            for j2 in range(2):
+                acc = acc_ps.tile([P, 512], F32, tag="acc")
+                c0 = jj * 512 + x * 256 + j2 * P
+                for g in range(PASSES):
+                    nc.tensor.matmul_mx(out=acc[:],
+                                        lhsT=wcodes[:, g, c0:c0 + P].bitcast(FP8X4), lhsT_scale=wscales[:, g, c0:c0 + P],
+                                        rhs=xcodes[:, g, tcols].bitcast(FP8X4), rhs_scale=xscales[:, g, tcols],
+                                        start=(g == 0), stop=(g == PASSES - 1))
+                if x == 0:
+                    ms_t = msrp.tile([P, 512], F32, tag="msr")
+                else:
+                    ms_t = mspp.tile([P, 512], F32, tag="msp")
+                ms[(jj, th, x, j2)] = ms_t
+                bc = x * 8 + 2 * jj + j2
+                nc.scalar.activation(out=ms_t[:], in_=acc[:], func=ACT.Identity, bias=bias_col[:, bc:bc + 1], scale=1.0)
+
+        def mx_tokens(jj, th):
+            c0 = jj * 512 + 256
+            for sb in range(2):
+                k = 2 * th + sb
+                acc = acc_ps.tile([P, 2, 256], F32, tag="acc")
+                for b in range(2):
+                    t0 = (k * 2 + b) * P
+                    for g in range(PASSES):
+                        nc.tensor.matmul_mx(out=acc[:, b, :],
+                                            lhsT=xcodes[:, g, t0:t0 + P].bitcast(FP8X4), lhsT_scale=xscales[:, g, t0:t0 + P],
+                                            rhs=wcodes[:, g, c0:c0 + 256].bitcast(FP8X4), rhs_scale=wscales[:, g, c0:c0 + 256],
+                                            start=(g == 0), stop=(g == PASSES - 1))
+                ot_t = otp.tile([P, 8, P], F32, tag="ot")
+                ot[(jj, k)] = ot_t
+                bv = bfull[:].rearrange("p (h x f) -> p h x f", x=2, f=64)[:, 4 * jj:4 * jj + 4, 1, :]
+                nc.vector.tensor_tensor(out=ot_t[:, :, 64:128].rearrange("p (b h) f -> p b h f", b=2),
+                                        in0=acc[:].rearrange("p b (h f) -> p b h f", f=64),
+                                        in1=bv.unsqueeze(1).to_broadcast([P, 2, 4, 64]), op=ALU.add)
+
+        def back(jj, th, x):
+            rot = 0
+            if x == 0:
+                rot = 8 if jj < 3 else 4
+            bkv = []
+            oxs = []
+            for sb in range(2):
+                k = 2 * th + sb
+                if x == 0 and jj == 3:
+                    ot_t = otp.tile([P, 8, P], F32, tag="ot")
+                    ot[(jj, k)] = ot_t
+                bk = back_ps.tile([P, 4, P], F32, tag="bk")
+                for b in range(2):
+                    for j2 in range(2):
+                        slot = b * 2 + j2 if jj < 3 else j2 * 2 + b
+                        t0 = (sb * 2 + b) * P
+                        nc.tensor.transpose(bk[:, slot, :], ms[(jj, th, x, j2)][:, t0:t0 + P], ident[:])
+                bkv.append(bk[:].rearrange("p s (a f) -> p (s a) f", a=2))
+                oxs.append(ot[(jj, k)][:, :, x * 64:(x + 1) * 64])
+            pqs = []
+            if rot > 0:
+                for sb in range(2):
+                    k = 2 * th + sb
+                    pq = pqp.tile([P, 2, 8, 64], F32, tag="pq")
+                    pqs.append(pq)
+                    nc.vector.tensor_tensor(out=pq[:, :, 0:rot, :],
+                                            in0=bkv[sb][:, 0:rot, :].unsqueeze(1).to_broadcast([P, 2, rot, 64]),
+                                            in1=tab[:, k, :, :].unsqueeze(2).to_broadcast([P, 2, rot, 64]), op=ALU.mult)
+            for sb in range(2):
+                k = 2 * th + sb
+                if rot < 8:
+                    nc.scalar.copy(out=oxs[sb][:, rot:8, :], in_=bkv[sb][:, rot:8, :])
+                if rot > 0:
+                    nc.gpsimd.tensor_tensor(out=oxs[sb][:, 0:rot, :].rearrange("p r (i e) -> p r i e", e=2),
+                                            in0=pqs[sb][:, 0, 0:rot, :].rearrange("p r (i e) -> p r i e", e=2),
+                                            in1=pqs[sb][:, 1, 0:rot, :].rearrange("p r (i e) -> p r i e", e=2)[:, :, :, ::-1],
+                                            op=ALU.add)
+                if x == 1 or jj < 3:
+                    o = ot[(jj, k)]
+                    rows = slice(k * P, (k + 1) * P)
+                    if jj < 3:
+                        nc.sync.dma_start(out=out_0[rows, :, 4 * jj:4 * jj + 4, :], in_=o[:].rearrange("p (b h) f -> p b h f", b=2))
+                    else:
+                        nc.sync.dma_start(out=out_1[rows, :, :, :], in_=o[:, 0:4, :].rearrange("p (b h) f -> p b h f", b=2))
+                        nc.sync.dma_start(out=out_2[rows, :, :, :], in_=o[:, 4:8, :].rearrange("p (b h) f -> p b h f", b=2))
+
+        allg = [0, 1, 2]
+        first = ORDER[0]
+        w_widen(first, 0)
+        w_widen(first, 1)
+        x_prep(0)
+        x_prep(1)
+        w_turn(first, 0, allg)
+        x_quant(0)
+        tables()
+        x_prep(2)
+        w_turn(first, 1, allg)
+        bias_turn()
+        w_quant(first, allg)
+        x_prep(3)
+        x_quant(1)
+        w_widen(ORDER[1], 0)
+        w_widen(ORDER[1], 1)
+
+        subs = [(jj, th, x) for jj in ORDER for th in range(2) for x in range(2)]
+        for n in range(len(subs)):
+            if subs[n][0] < 3 and subs[n][2] == 1:
+                mx_tokens(subs[n][0], subs[n][1])
+            else:
+                mx(*subs[n])
+            if n > 0 and (subs[n - 1][0] == 3 or subs[n - 1][2] == 0):
+                back(*subs[n - 1])
+            m = n // 4 + 1
+            i = n % 4
+            if m < 4 and i < 3:
+                w_turn(ORDER[m], 0, [i])
+                w_turn(ORDER[m], 1, [i])
+                w_quant(ORDER[m], [i])
+            if m + 1 < 4 and i in (1, 2):
+                w_widen(ORDER[m + 1], i - 1)

@@ -37,6 +37,14 @@ def tile_selfattention_pa_kernel(tc, hidden_states, rotary_pos_emb, W_qkv_bytes,
         back_ps = ctx.enter_context(tc.psum_pool(name="back_ps", bufs=3))
         ctx.enter_context(tc.manual_schedule(engines={mybir.EngineType.PE}))
 
+        wz = const.tile([P, 512], BF16, tag="wz")
+        nc.vector.memset(wz[:], 0.0)
+
+        def warm(n):
+            wp = acc_ps.tile([P, 512], F32, tag="acc")
+            for i in range(n):
+                nc.tensor.matmul(wp[:], lhsT=wz[:, 0:P], rhs=wz[:], start=True, stop=True)
+
         sc = const.tile([P, K], F32, tag="sc")
         nc.scalar.dma_start(out=sc[:], in_=W_qkv_scale.rearrange("o k -> (o k)").partition_broadcast(P))
         wb = {}
@@ -241,16 +249,22 @@ def tile_selfattention_pa_kernel(tc, hidden_states, rotary_pos_emb, W_qkv_bytes,
 
         allg = [0, 1, 2]
         first = ORDER[0]
+        warm(16)
         w_widen(first, 0)
         w_widen(first, 1)
         x_prep(0)
+        warm(2)
         x_prep(1)
+        warm(2)
         w_turn(first, 0, allg)
+        warm(2)
         x_quant(0)
         tables()
         x_prep(2)
+        warm(2)
         w_turn(first, 1, allg)
         bias_turn()
+        warm(2)
         w_quant(first, allg)
         x_prep(3)
         x_quant(1)

@@ -45,8 +45,24 @@ def tile_selfattention_pa_kernel(tc, hidden_states, rotary_pos_emb, W_qkv_bytes,
             for i in range(n):
                 nc.tensor.matmul(wp[:], lhsT=wz[:, 0:P], rhs=wz[:], start=True, stop=True)
 
+        srow = const.tile([P, P], F32, tag="srow")
+        nc.gpsimd.memset(srow[:], 0.0)
+        nc.sync.dma_start(out=srow[0:K // P, :], in_=W_qkv_scale.rearrange("o (c p) -> (o c) p", p=P))
+        ident = const.tile([P, P], F32, tag="ident")
+        make_identity(nc, ident[:])
+        sccol = const.tile([P, K // P], F32, tag="sccol")
         sc = const.tile([P, K], F32, tag="sc")
-        nc.scalar.dma_start(out=sc[:], in_=W_qkv_scale.rearrange("o k -> (o k)").partition_broadcast(P))
+
+        def scales_spread():
+            st = prep_ps.tile([P, P], F32, tag="prep")
+            nc.tensor.transpose(st[:], srow[:], ident[:])
+            nc.scalar.copy(out=sccol[:], in_=st[:, 0:K // P])
+            for c3 in range(PASSES):
+                sp = prep_ps.tile([P, 4, P], F32, tag="prep")
+                for c in range(4):
+                    nc.tensor.transpose(sp[:, c, :], sccol[:, 4 * c3 + c:4 * c3 + c + 1].to_broadcast([P, P]), ident[:])
+                nc.scalar.copy(out=sc[:, c3 * 512:(c3 + 1) * 512], in_=sp[:].rearrange("p c n -> p (c n)"))
+
         wb = {}
         xraw = []
 
@@ -79,8 +95,6 @@ def tile_selfattention_pa_kernel(tc, hidden_states, rotary_pos_emb, W_qkv_bytes,
         for x in range(2):
             nc.scalar.dma_start(out=brow[x * 8:(x + 1) * 8, :].rearrange("j (a f) -> j a f", a=2), in_=bview[x])
 
-        ident = const.tile([P, P], F32, tag="ident")
-        make_identity(nc, ident[:])
         identb = const.tile([P, P], BF16, tag="identb")
         make_identity(nc, identb[:])
 
@@ -137,7 +151,11 @@ def tile_selfattention_pa_kernel(tc, hidden_states, rotary_pos_emb, W_qkv_bytes,
             wbf_t = rawp.tile([P, 2, K], BF16, tag="raw")
             wbf[(jj, j2)] = wbf_t
             for a in range(2):
-                nc.vector.tensor_tensor(out=wbf_t[:, a, :], in0=wb[(jj, j2)][:, a, :].bitcast(FP8), in1=sc[:], op=ALU.mult)
+                pieces = PASSES if (jj, j2, a) == (ORDER[0], 0, 0) else 1
+                w = K // pieces
+                for c in range(pieces):
+                    nc.vector.tensor_tensor(out=wbf_t[:, a, c * w:(c + 1) * w], in0=wb[(jj, j2)][:, a, c * w:(c + 1) * w].bitcast(FP8),
+                                            in1=sc[:, c * w:(c + 1) * w], op=ALU.mult)
 
         def w_turn(jj, j2, gs):
             if jj not in wg:
@@ -182,6 +200,26 @@ def tile_selfattention_pa_kernel(tc, hidden_states, rotary_pos_emb, W_qkv_bytes,
                 bc = x * 8 + 2 * jj + j2
                 nc.scalar.activation(out=ms_t[:], in_=acc[:], func=ACT.Identity, bias=bias_col[:, bc:bc + 1], scale=1.0)
 
+        halves = {}
+
+        def get_ot(jj, k):
+            if (jj, k) not in ot:
+                ot_t = otp.tile([P, 8, P], F32, tag="ot")
+                ot[(jj, k)] = ot_t
+                halves[(jj, k)] = 0
+            return ot[(jj, k)]
+
+        def half_done(jj, k):
+            halves[(jj, k)] = halves[(jj, k)] + 1
+            if halves[(jj, k)] == 2:
+                o = ot[(jj, k)]
+                rows = slice(k * P, (k + 1) * P)
+                if jj < 3:
+                    nc.sync.dma_start(out=out_0[rows, :, 4 * jj:4 * jj + 4, :], in_=o[:].rearrange("p (b h) f -> p b h f", b=2))
+                else:
+                    nc.sync.dma_start(out=out_1[rows, :, :, :], in_=o[:, 0:4, :].rearrange("p (b h) f -> p b h f", b=2))
+                    nc.sync.dma_start(out=out_2[rows, :, :, :], in_=o[:, 4:8, :].rearrange("p (b h) f -> p b h f", b=2))
+
         def mx_tokens(jj, th):
             c0 = jj * 512 + 256
             for sb in range(2):
@@ -194,12 +232,12 @@ def tile_selfattention_pa_kernel(tc, hidden_states, rotary_pos_emb, W_qkv_bytes,
                                             lhsT=xcodes[:, g, t0:t0 + P].bitcast(FP8X4), lhsT_scale=xscales[:, g, t0:t0 + P],
                                             rhs=wcodes[:, g, c0:c0 + 256].bitcast(FP8X4), rhs_scale=wscales[:, g, c0:c0 + 256],
                                             start=(g == 0), stop=(g == PASSES - 1))
-                ot_t = otp.tile([P, 8, P], F32, tag="ot")
-                ot[(jj, k)] = ot_t
+                ot_t = get_ot(jj, k)
                 bv = bfull[:].rearrange("p (h x f) -> p h x f", x=2, f=64)[:, 4 * jj:4 * jj + 4, 1, :]
                 nc.vector.tensor_tensor(out=ot_t[:, :, 64:128].rearrange("p (b h) f -> p b h f", b=2),
                                         in0=acc[:].rearrange("p b (h f) -> p b h f", f=64),
                                         in1=bv.unsqueeze(1).to_broadcast([P, 2, 4, 64]), op=ALU.add)
+                half_done(jj, k)
 
         def back(jj, th, x):
             rot = 0
@@ -209,9 +247,7 @@ def tile_selfattention_pa_kernel(tc, hidden_states, rotary_pos_emb, W_qkv_bytes,
             oxs = []
             for sb in range(2):
                 k = 2 * th + sb
-                if x == 0 and jj == 3:
-                    ot_t = otp.tile([P, 8, P], F32, tag="ot")
-                    ot[(jj, k)] = ot_t
+                get_ot(jj, k)
                 bk = back_ps.tile([P, 4, P], F32, tag="bk")
                 for b in range(2):
                     for j2 in range(2):
@@ -238,18 +274,13 @@ def tile_selfattention_pa_kernel(tc, hidden_states, rotary_pos_emb, W_qkv_bytes,
                                             in0=pqs[sb][:, 0, 0:rot, :].rearrange("p r (i e) -> p r i e", e=2),
                                             in1=pqs[sb][:, 1, 0:rot, :].rearrange("p r (i e) -> p r i e", e=2)[:, :, :, ::-1],
                                             op=ALU.add)
-                if x == 1 or jj < 3:
-                    o = ot[(jj, k)]
-                    rows = slice(k * P, (k + 1) * P)
-                    if jj < 3:
-                        nc.sync.dma_start(out=out_0[rows, :, 4 * jj:4 * jj + 4, :], in_=o[:].rearrange("p (b h) f -> p b h f", b=2))
-                    else:
-                        nc.sync.dma_start(out=out_1[rows, :, :, :], in_=o[:, 0:4, :].rearrange("p (b h) f -> p b h f", b=2))
-                        nc.sync.dma_start(out=out_2[rows, :, :, :], in_=o[:, 4:8, :].rearrange("p (b h) f -> p b h f", b=2))
+                half_done(jj, k)
 
         allg = [0, 1, 2]
         first = ORDER[0]
-        warm(16)
+        warm(3)
+        scales_spread()
+        warm(2)
         w_widen(first, 0)
         w_widen(first, 1)
         x_prep(0)
@@ -271,7 +302,8 @@ def tile_selfattention_pa_kernel(tc, hidden_states, rotary_pos_emb, W_qkv_bytes,
         w_widen(ORDER[1], 0)
         w_widen(ORDER[1], 1)
 
-        subs = [(jj, th, x) for jj in ORDER for th in range(2) for x in range(2)]
+        subs = [(jj, th, x) for jj in ORDER[:3] for th in range(2) for x in range(2)]
+        subs = subs + [(ORDER[3], th, x) for x in range(2) for th in range(2)]
         for n in range(len(subs)):
             if subs[n][0] < 3 and subs[n][2] == 1:
                 mx_tokens(subs[n][0], subs[n][1])

@@ -35,7 +35,7 @@ def tile_selfattention_pa_kernel(tc, hidden_states, rotary_pos_emb, W_qkv_bytes,
         prep_ps = ctx.enter_context(tc.psum_pool(name="prep_ps", bufs=2))
         acc_ps = ctx.enter_context(tc.psum_pool(name="acc_ps", bufs=3))
         back_ps = ctx.enter_context(tc.psum_pool(name="back_ps", bufs=3))
-        ctx.enter_context(tc.manual_schedule(engines={mybir.EngineType.PE}))
+        ctx.enter_context(tc.manual_schedule(engines={mybir.EngineType.PE, mybir.EngineType.SP}))
 
         wz = const.tile([P, 512], BF16, tag="wz")
         nc.vector.memset(wz[:], 0.0)
@@ -45,23 +45,18 @@ def tile_selfattention_pa_kernel(tc, hidden_states, rotary_pos_emb, W_qkv_bytes,
             for i in range(n):
                 nc.tensor.matmul(wp[:], lhsT=wz[:, 0:P], rhs=wz[:], start=True, stop=True)
 
-        srow = const.tile([P, P], F32, tag="srow")
-        nc.gpsimd.memset(srow[:], 0.0)
-        nc.sync.dma_start(out=srow[0:K // P, :], in_=W_qkv_scale.rearrange("o (c p) -> (o c) p", p=P))
+        sccol = const.tile([P, PASSES, 4], F32, tag="sccol")
+        nc.sync.dma_start(out=sccol[:], in_=W_qkv_scale.rearrange("o (g p t) -> p (o g) t", p=P, t=4))
         ident = const.tile([P, P], F32, tag="ident")
         make_identity(nc, ident[:])
-        sccol = const.tile([P, K // P], F32, tag="sccol")
         sc = const.tile([P, K], F32, tag="sc")
 
         def scales_spread():
-            st = prep_ps.tile([P, P], F32, tag="prep")
-            nc.tensor.transpose(st[:], srow[:], ident[:])
-            nc.scalar.copy(out=sccol[:], in_=st[:, 0:K // P])
-            for c3 in range(PASSES):
+            for g in range(PASSES):
                 sp = prep_ps.tile([P, 4, P], F32, tag="prep")
-                for c in range(4):
-                    nc.tensor.transpose(sp[:, c, :], sccol[:, 4 * c3 + c:4 * c3 + c + 1].to_broadcast([P, P]), ident[:])
-                nc.scalar.copy(out=sc[:, c3 * 512:(c3 + 1) * 512], in_=sp[:].rearrange("p c n -> p (c n)"))
+                for t in range(4):
+                    nc.tensor.transpose(sp[:, t, :], sccol[:, g, t:t + 1].to_broadcast([P, P]), ident[:])
+                nc.scalar.copy(out=sc[:, g * 512:(g + 1) * 512].rearrange("p (n t) -> p n t", t=4), in_=sp[:].rearrange("p t n -> p n t"))
 
         wb = {}
         xraw = []
@@ -100,7 +95,6 @@ def tile_selfattention_pa_kernel(tc, hidden_states, rotary_pos_emb, W_qkv_bytes,
 
         tab = const.tile([P, 4, 2, 64], F32, tag="tab")
         bfull = const.tile([P, 2048], BF16, tag="bfull")
-        nc.sync.dma_start(out=bfull[:], in_=b_qkv.partition_broadcast(P))
         bias_col = const.tile([P, 16], F32, tag="bias_col")
 
         def tables():
@@ -311,6 +305,8 @@ def tile_selfattention_pa_kernel(tc, hidden_states, rotary_pos_emb, W_qkv_bytes,
                 mx(*subs[n])
             if n > 0 and (subs[n - 1][0] == 3 or subs[n - 1][2] == 0):
                 back(*subs[n - 1])
+            if n == 2:
+                nc.sync.dma_start(out=bfull[:], in_=b_qkv.partition_broadcast(P))
             m = n // 4 + 1
             i = n % 4
             if m < 4 and i < 3:

@@ -264,7 +264,8 @@ def tile_selfattention_pa_kernel(tc, hidden_states, rotary_pos_emb, W_qkv_bytes,
                 if rot < 8:
                     nc.scalar.copy(out=oxs[sb][:, rot:8, :], in_=bkv[sb][:, rot:8, :])
                 if rot > 0:
-                    nc.gpsimd.tensor_tensor(out=oxs[sb][:, 0:rot, :].rearrange("p r (i e) -> p r i e", e=2),
+                    eng = nc.vector if jj in ORDER[:2] else nc.gpsimd
+                    eng.tensor_tensor(out=oxs[sb][:, 0:rot, :].rearrange("p r (i e) -> p r i e", e=2),
                                             in0=pqs[sb][:, 0, 0:rot, :].rearrange("p r (i e) -> p r i e", e=2),
                                             in1=pqs[sb][:, 1, 0:rot, :].rearrange("p r (i e) -> p r i e", e=2)[:, :, :, ::-1],
                                             op=ALU.add)

@@ -32,16 +32,16 @@ def tile_selfattention_pa_kernel(tc, hidden_states, rotary_pos_emb, W_qkv_bytes,
         mspp = ctx.enter_context(tc.tile_pool(name="mspp", bufs=4))
         pqp = ctx.enter_context(tc.tile_pool(name="pqp", bufs=3))
         otp = ctx.enter_context(tc.tile_pool(name="otp", bufs=6))
-        prep_ps = ctx.enter_context(tc.psum_pool(name="prep_ps", bufs=2))
-        acc_ps = ctx.enter_context(tc.psum_pool(name="acc_ps", bufs=3))
-        back_ps = ctx.enter_context(tc.psum_pool(name="back_ps", bufs=3))
+        prep_ps = ctx.enter_context(tc.psum_pool(name="work_ps", bufs=8))
+        acc_ps = prep_ps
+        back_ps = prep_ps
         ctx.enter_context(tc.manual_schedule(engines={mybir.EngineType.PE, mybir.EngineType.SP}))
 
         wz = const.tile([P, 512], BF16, tag="wz")
         nc.vector.memset(wz[:], 0.0)
 
         def warm(n):
-            wp = acc_ps.tile([P, 512], F32, tag="acc")
+            wp = acc_ps.tile([P, 512], F32, tag="ps")
             for i in range(n):
                 nc.tensor.matmul(wp[:], lhsT=wz[:, 0:P], rhs=wz[:], start=True, stop=True)
 
@@ -53,7 +53,7 @@ def tile_selfattention_pa_kernel(tc, hidden_states, rotary_pos_emb, W_qkv_bytes,
 
         def scales_spread():
             for g in range(PASSES):
-                sp = prep_ps.tile([P, 4, P], F32, tag="prep")
+                sp = prep_ps.tile([P, 4, P], F32, tag="ps")
                 for t in range(4):
                     nc.tensor.transpose(sp[:, t, :], sccol[:, g, t:t + 1].to_broadcast([P, P]), ident[:])
                 nc.scalar.copy(out=sc[:, g * 512:(g + 1) * 512].rearrange("p (n t) -> p n t", t=4), in_=sp[:].rearrange("p t n -> p n t"))
@@ -107,7 +107,7 @@ def tile_selfattention_pa_kernel(tc, hidden_states, rotary_pos_emb, W_qkv_bytes,
             nc.scalar.activation(out=snv[:, :, :, 1], in_=rpv[:, :, :, 1], func=ACT.Copy, scale=-1.0)
 
         def bias_turn():
-            bt_ps = prep_ps.tile([P, P], BF16, tag="prep")
+            bt_ps = prep_ps.tile([P, P], BF16, tag="ps")
             nc.tensor.transpose(bt_ps[:], brow[:], identb[:])
             nc.scalar.copy(out=bias_col[:], in_=bt_ps[:, 0:16])
 
@@ -128,7 +128,7 @@ def tile_selfattention_pa_kernel(tc, hidden_states, rotary_pos_emb, W_qkv_bytes,
             words = xraw[k][:].rearrange("p b k -> p (b k)").bitcast(F32)
             xgw = xg[th][:].bitcast(F32)
             for g in range(PASSES):
-                xt = prep_ps.tile([P, 2, 256], F32, tag="prep")
+                xt = prep_ps.tile([P, 2, 256], F32, tag="ps")
                 for b in range(2):
                     for u in range(2):
                         lo = b * KW + 256 * g
@@ -158,7 +158,7 @@ def tile_selfattention_pa_kernel(tc, hidden_states, rotary_pos_emb, W_qkv_bytes,
             words = wbf[(jj, j2)][:].rearrange("p a k -> p (a k)").bitcast(F32)
             wgw = wg[jj][:].bitcast(F32)
             for g in gs:
-                wt = prep_ps.tile([P, 2, 256], F32, tag="prep")
+                wt = prep_ps.tile([P, 2, 256], F32, tag="ps")
                 for a in range(2):
                     for u in range(2):
                         lo = a * KW + 256 * g
@@ -179,7 +179,7 @@ def tile_selfattention_pa_kernel(tc, hidden_states, rotary_pos_emb, W_qkv_bytes,
         def mx(jj, th, x):
             tcols = slice(th * 512, (th + 1) * 512)
             for j2 in range(2):
-                acc = acc_ps.tile([P, 512], F32, tag="acc")
+                acc = acc_ps.tile([P, 512], F32, tag="ps")
                 c0 = jj * 512 + x * 256 + j2 * P
                 for g in range(PASSES):
                     nc.tensor.matmul_mx(out=acc[:],
@@ -218,7 +218,7 @@ def tile_selfattention_pa_kernel(tc, hidden_states, rotary_pos_emb, W_qkv_bytes,
             c0 = jj * 512 + 256
             for sb in range(2):
                 k = 2 * th + sb
-                acc = acc_ps.tile([P, 2, 256], F32, tag="acc")
+                acc = acc_ps.tile([P, 2, 256], F32, tag="ps")
                 for b in range(2):
                     t0 = (k * 2 + b) * P
                     for g in range(PASSES):
@@ -242,7 +242,7 @@ def tile_selfattention_pa_kernel(tc, hidden_states, rotary_pos_emb, W_qkv_bytes,
             for sb in range(2):
                 k = 2 * th + sb
                 get_ot(jj, k)
-                bk = back_ps.tile([P, 4, P], F32, tag="bk")
+                bk = back_ps.tile([P, 4, P], F32, tag="ps")
                 for b in range(2):
                     for j2 in range(2):
                         slot = b * 2 + j2 if jj < 3 else j2 * 2 + b

@@ -38,7 +38,10 @@ def tile_selfattention_pa_kernel(tc, hidden_states, rotary_pos_emb, W_qkv_bytes,
         ctx.enter_context(tc.manual_schedule(engines={mybir.EngineType.PE, mybir.EngineType.SP}))
 
         wz = const.tile([P, 512], BF16, tag="wz")
-        nc.vector.memset(wz[:], 0.0)
+        nc.vector.memset(wz[:, 0:2], 0.0)
+        first_act = const.tile([P, 2], BF16, tag="first_act")
+        nc.scalar.copy(out=first_act[:], in_=wz[:, 0:2])
+        nc.vector.memset(wz[:, 2:512], 0.0)
 
         def warm(n):
             wp = acc_ps.tile([P, 512], F32, tag="ps")
@@ -56,7 +59,10 @@ def tile_selfattention_pa_kernel(tc, hidden_states, rotary_pos_emb, W_qkv_bytes,
                 sp = prep_ps.tile([P, 4, P], F32, tag="ps")
                 for t in range(4):
                     nc.tensor.transpose(sp[:, t, :], sccol[:, g, t:t + 1].to_broadcast([P, P]), ident[:])
-                nc.scalar.copy(out=sc[:, g * 512:(g + 1) * 512].rearrange("p (n t) -> p n t", t=4), in_=sp[:].rearrange("p t n -> p n t"))
+                if g == 0:
+                    nc.vector.tensor_copy(out=sc[:, g * 512:(g + 1) * 512].rearrange("p (n t) -> p n t", t=4), in_=sp[:].rearrange("p t n -> p n t"))
+                else:
+                    nc.scalar.copy(out=sc[:, g * 512:(g + 1) * 512].rearrange("p (n t) -> p n t", t=4), in_=sp[:].rearrange("p t n -> p n t"))
 
         wb = {}
         xraw = []

@@ -168,11 +168,9 @@ def tile_selfattention_pa_kernel(tc, hidden_states, rotary_pos_emb, W_qkv_bytes,
                 for a in range(2):
                     for u in range(2):
                         lo = a * KW + 256 * g
-                        nc.tensor.transpose(wt[:, u, a * P:(a + 1) * P], words[:, lo + u:lo + 256:2], ident[:])
-                wtv = wt[:].rearrange("p u (a x f) -> p x a f u", a=2, x=2)
-                for x in range(2):
-                    lo = x * 512 + j2 * 256
-                    nc.scalar.copy(out=wgw[:, g, lo:lo + 256].rearrange("p (a f u) -> p a f u", a=2, u=2), in_=wtv[:, x])
+                        nc.tensor.transpose(wt[:, u, :].rearrange("p (x a f) -> p x a f", x=2, a=2)[:, :, a, :], words[:, lo + u:lo + 256:2], ident[:])
+                nc.scalar.copy(out=wgw[:, g, :].rearrange("p (x j c u) -> p x j c u", x=2, j=2, u=2)[:, :, j2],
+                               in_=wt[:].rearrange("p u (x c) -> p x c u", x=2))
 
         def w_quant(jj, gs):
             for g in gs:
@@ -220,10 +218,28 @@ def tile_selfattention_pa_kernel(tc, hidden_states, rotary_pos_emb, W_qkv_bytes,
                     nc.sync.dma_start(out=out_1[rows, :, :, :], in_=o[:, 0:4, :].rearrange("p (b h) f -> p b h f", b=2))
                     nc.sync.dma_start(out=out_2[rows, :, :, :], in_=o[:, 4:8, :].rearrange("p (b h) f -> p b h f", b=2))
 
+        def last_tile(jj, k):
+            c0 = jj * 512 + 256
+            ot_t = get_ot(jj, k)
+            bv = bfull[:].rearrange("p (h x f) -> p h x f", x=2, f=64)[:, 4 * jj:4 * jj + 4, 1, :]
+            for b in range(2):
+                acc = acc_ps.tile([P, 256], F32, tag="ps")
+                t0 = (k * 2 + b) * P
+                for g in range(PASSES):
+                    nc.tensor.matmul_mx(out=acc[:],
+                                        lhsT=xcodes[:, g, t0:t0 + P].bitcast(FP8X4), lhsT_scale=xscales[:, g, t0:t0 + P],
+                                        rhs=wcodes[:, g, c0:c0 + 256].bitcast(FP8X4), rhs_scale=wscales[:, g, c0:c0 + 256],
+                                        start=(g == 0), stop=(g == PASSES - 1))
+                nc.vector.tensor_tensor(out=ot_t[:, 4 * b:4 * b + 4, 64:128], in0=acc[:].rearrange("p (h f) -> p h f", f=64), in1=bv, op=ALU.add)
+                nc.sync.dma_start(out=out_0[k * P:(k + 1) * P, b, 4 * jj:4 * jj + 4, :], in_=ot_t[:, 4 * b:4 * b + 4, :])
+
         def mx_tokens(jj, th):
             c0 = jj * 512 + 256
             for sb in range(2):
                 k = 2 * th + sb
+                if (jj, k) == (ORDER[3], 3):
+                    last_tile(jj, k)
+                    continue
                 acc = acc_ps.tile([P, 2, 256], F32, tag="ps")
                 for b in range(2):
                     t0 = (k * 2 + b) * P

@@ -31,11 +31,12 @@ def tile_selfattention_pa_kernel(tc, hidden_states, rotary_pos_emb, W_qkv_bytes,
         msrp = ctx.enter_context(tc.tile_pool(name="msrp", bufs=4))
         mspp = ctx.enter_context(tc.tile_pool(name="mspp", bufs=4))
         pqp = ctx.enter_context(tc.tile_pool(name="pqp", bufs=3))
-        otp = ctx.enter_context(tc.tile_pool(name="otp", bufs=6))
+        qdp = ctx.enter_context(tc.tile_pool(name="qdp", bufs=4))
+        otp = ctx.enter_context(tc.tile_pool(name="otp", bufs=10))
         prep_ps = ctx.enter_context(tc.psum_pool(name="work_ps", bufs=8))
         acc_ps = prep_ps
         back_ps = prep_ps
-        ctx.enter_context(tc.manual_schedule(engines={mybir.EngineType.PE, mybir.EngineType.SP}))
+        ctx.enter_context(tc.manual_schedule(engines={mybir.EngineType.PE, mybir.EngineType.SP, mybir.EngineType.Pool}))
 
         wz = const.tile([P, 512], BF16, tag="wz")
         nc.vector.memset(wz[:, 0:2], 0.0)
@@ -218,6 +219,8 @@ def tile_selfattention_pa_kernel(tc, hidden_states, rotary_pos_emb, W_qkv_bytes,
                     nc.sync.dma_start(out=out_1[rows, :, :, :], in_=o[:, 0:4, :].rearrange("p (b h) f -> p b h f", b=2))
                     nc.sync.dma_start(out=out_2[rows, :, :, :], in_=o[:, 4:8, :].rearrange("p (b h) f -> p b h f", b=2))
 
+        late_bias = []
+
         def last_tile(jj, k):
             c0 = jj * 512 + 256
             ot_t = get_ot(jj, k)
@@ -250,9 +253,27 @@ def tile_selfattention_pa_kernel(tc, hidden_states, rotary_pos_emb, W_qkv_bytes,
                                             start=(g == 0), stop=(g == PASSES - 1))
                 ot_t = get_ot(jj, k)
                 bv = bfull[:].rearrange("p (h x f) -> p h x f", x=2, f=64)[:, 4 * jj:4 * jj + 4, 1, :]
-                nc.vector.tensor_tensor(out=ot_t[:, :, 64:128].rearrange("p (b h) f -> p b h f", b=2),
-                                        in0=acc[:].rearrange("p b (h f) -> p b h f", f=64),
-                                        in1=bv.unsqueeze(1).to_broadcast([P, 2, 4, 64]), op=ALU.add)
+                ov = ot_t[:, :, 64:128].rearrange("p (b h) f -> p b h f", b=2)
+                if jj == ORDER[1]:
+                    nc.scalar.copy(out=ov, in_=acc[:].rearrange("p b (h f) -> p b h f", f=64))
+                    late_bias.append((jj, k, ov, bv))
+                else:
+                    nc.vector.tensor_tensor(out=ov, in0=acc[:].rearrange("p b (h f) -> p b h f", f=64),
+                                            in1=bv.unsqueeze(1).to_broadcast([P, 2, 4, 64]), op=ALU.add)
+                    half_done(jj, k)
+
+        late = []
+        fence = const.tile([P, 2], BF16, tag="fence")
+
+        def late_adds():
+            while len(late) > 0:
+                jj, k, ox, qd = late.pop(0)
+                nc.gpsimd.tensor_tensor(out=ox.rearrange("p r (i e) -> p r i e", e=2), in0=ox.rearrange("p r (i e) -> p r i e", e=2),
+                                        in1=qd[:].rearrange("p r (i e) -> p r i e", e=2)[:, :, :, ::-1], op=ALU.add)
+                half_done(jj, k)
+            while len(late_bias) > 0:
+                jj, k, ov, bv = late_bias.pop(0)
+                nc.gpsimd.tensor_tensor(out=ov, in0=ov, in1=bv.unsqueeze(1).to_broadcast([P, 2, 4, 64]), op=ALU.add)
                 half_done(jj, k)
 
         def back(jj, th, x):
@@ -273,6 +294,14 @@ def tile_selfattention_pa_kernel(tc, hidden_states, rotary_pos_emb, W_qkv_bytes,
                 bkv.append(bk[:].rearrange("p s (a f) -> p (s a) f", a=2))
                 oxs.append(ot[(jj, k)][:, :, x * 64:(x + 1) * 64])
             pqs = []
+            if jj == ORDER[1]:
+                for sb in range(2):
+                    k = 2 * th + sb
+                    qd = qdp.tile([P, 8, 64], F32, tag="qd")
+                    nc.vector.tensor_tensor(out=oxs[sb], in0=bkv[sb], in1=tab[:, k, 0, :].unsqueeze(1).to_broadcast([P, 8, 64]), op=ALU.mult)
+                    nc.vector.tensor_tensor(out=qd[:], in0=bkv[sb], in1=tab[:, k, 1, :].unsqueeze(1).to_broadcast([P, 8, 64]), op=ALU.mult)
+                    late.append((jj, k, oxs[sb], qd))
+                return
             if rot > 0:
                 for sb in range(2):
                     k = 2 * th + sb
@@ -338,3 +367,7 @@ def tile_selfattention_pa_kernel(tc, hidden_states, rotary_pos_emb, W_qkv_bytes,
                 w_quant(ORDER[m], [i])
             if m + 1 < 4 and i in (1, 2):
                 w_widen(ORDER[m + 1], i - 1)
+            if n == 6:
+                nc.gpsimd.tensor_copy(out=fence[:], in_=wbf[(ORDER[3], 1)][:, 1, K - 2:K])
+            if n in (6, 7):
+                late_adds()

@@ -152,7 +152,7 @@ def tile_selfattention_pa_kernel(tc, hidden_states, rotary_pos_emb, W_qkv_bytes,
             wbf_t = rawp.tile([P, 2, K], BF16, tag="raw")
             wbf[(jj, j2)] = wbf_t
             for a in range(2):
-                pieces = PASSES if (jj, j2, a) == (ORDER[0], 0, 0) else 1
+                pieces = PASSES if (jj, j2, a) == (ORDER[0], 0, 0) else 2
                 w = K // pieces
                 for c in range(pieces):
                     nc.vector.tensor_tensor(out=wbf_t[:, a, c * w:(c + 1) * w], in0=wb[(jj, j2)][:, a, c * w:(c + 1) * w].bitcast(FP8),

from contextlib import ExitStack

import concourse.mybir as mybir
from concourse.masks import make_identity

FLOPS = 2 * 1024 * 2048 * 1536

F32 = mybir.dt.float32
BF16 = mybir.dt.bfloat16
U32 = mybir.dt.uint32
U8 = mybir.dt.uint8
FP8 = mybir.dt.float8_e4m3fn
FP8X4 = mybir.dt.float8_e4m3fn_x4
ALU = mybir.AluOpType
ACT = mybir.ActivationFunctionType

P = 128
K = 1536
PASSES = 3
KW = K // 2
ORDER = [3, 0, 1, 2]


def tile_selfattention_pa_kernel(tc, hidden_states, rotary_pos_emb, W_qkv_bytes, W_qkv_scale, b_qkv, out_0, out_1, out_2):
    nc = tc.nc
    with ExitStack() as ctx:
        const = ctx.enter_context(tc.tile_pool(name="const", bufs=1))
        rawp = ctx.enter_context(tc.tile_pool(name="rawp", bufs=6))
        wbytes = ctx.enter_context(tc.tile_pool(name="wbytes", bufs=8))
        grpp = ctx.enter_context(tc.tile_pool(name="grpp", bufs=3))
        msrp = ctx.enter_context(tc.tile_pool(name="msrp", bufs=4))
        mspp = ctx.enter_context(tc.tile_pool(name="mspp", bufs=4))
        pqp = ctx.enter_context(tc.tile_pool(name="pqp", bufs=3))
        qdp = ctx.enter_context(tc.tile_pool(name="qdp", bufs=4))
        otp = ctx.enter_context(tc.tile_pool(name="otp", bufs=10))
        prep_ps = ctx.enter_context(tc.psum_pool(name="work_ps", bufs=8))
        acc_ps = prep_ps
        back_ps = prep_ps
        ctx.enter_context(tc.manual_schedule(engines={mybir.EngineType.PE, mybir.EngineType.SP, mybir.EngineType.Pool}))

        wz = const.tile([P, 512], BF16, tag="wz")
        nc.vector.memset(wz[:, 0:2], 0.0)
        first_act = const.tile([P, 2], BF16, tag="first_act")
        nc.scalar.copy(out=first_act[:], in_=wz[:, 0:2])
        nc.vector.memset(wz[:, 2:512], 0.0)

        def warm(n):
            wp = acc_ps.tile([P, 512], F32, tag="ps")
            for i in range(n):
                nc.tensor.matmul(wp[:], lhsT=wz[:, 0:P], rhs=wz[:], start=True, stop=True)

        sccol = const.tile([P, PASSES, 4], F32, tag="sccol")
        nc.sync.dma_start(out=sccol[:], in_=W_qkv_scale.rearrange("o (g p t) -> p (o g) t", p=P, t=4))
        ident = const.tile([P, P], F32, tag="ident")
        make_identity(nc, ident[:])
        sc = const.tile([P, K], F32, tag="sc")

        def scales_spread():
            for g in range(PASSES):
                sp = prep_ps.tile([P, 4, P], F32, tag="ps")
                for t in range(4):
                    nc.tensor.transpose(sp[:, t, :], sccol[:, g, t:t + 1].to_broadcast([P, P]), ident[:])
                if g == 0:
                    nc.vector.tensor_copy(out=sc[:, g * 512:(g + 1) * 512].rearrange("p (n t) -> p n t", t=4), in_=sp[:].rearrange("p t n -> p n t"))
                else:
                    nc.scalar.copy(out=sc[:, g * 512:(g + 1) * 512].rearrange("p (n t) -> p n t", t=4), in_=sp[:].rearrange("p t n -> p n t"))

        wb = {}
        xraw = []

        def load_w(jj, j2):
            wb_t = wbytes.tile([P, 2, K], U8, tag="wb")
            wb[(jj, j2)] = wb_t
            r0 = jj * 512 + j2 * 256
            nc.sync.dma_start(out=wb_t[:], in_=W_qkv_bytes[r0:r0 + 256, :].rearrange("(c p) k -> p c k", p=P))

        def load_x(k):
            xraw_t = rawp.tile([P, 2, K], BF16, tag="raw")
            xraw.append(xraw_t)
            nc.sync.dma_start(out=xraw_t[:], in_=hidden_states[k * P:(k + 1) * P, :, :])

        load_w(ORDER[0], 0)
        load_x(0)
        load_w(ORDER[0], 1)
        load_x(1)
        load_x(2)
        load_x(3)
        for jj in ORDER[1:]:
            load_w(jj, 0)
            load_w(jj, 1)

        rp = const.tile([P, 4, 64], BF16, tag="rp")
        nc.scalar.dma_start(out=rp[:], in_=rotary_pos_emb.rearrange("(k p) o i e -> p k (o i e)", p=P))
        brow = const.tile([P, P], BF16, tag="brow")
        nc.gpsimd.memset(brow[:], 0.0)
        bview = b_qkv.rearrange("(j a x f) -> x j a f", j=8, a=2, x=2, f=64)
        for x in range(2):
            nc.scalar.dma_start(out=brow[x * 8:(x + 1) * 8, :].rearrange("j (a f) -> j a f", a=2), in_=bview[x])

        identb = const.tile([P, P], BF16, tag="identb")
        make_identity(nc, identb[:])

        tab = const.tile([P, 4, 2, 64], F32, tag="tab")
        bfull = const.tile([P, 2048], BF16, tag="bfull")
        bias_col = const.tile([P, 16], F32, tag="bias_col")

        def tables():
            rpv = rp[:].rearrange("p k (i e) -> p k i e", e=2)
            c2v = tab[:, :, 0, :].rearrange("p k (i e) -> p k i e", e=2)
            snv = tab[:, :, 1, :].rearrange("p k (i e) -> p k i e", e=2)
            nc.scalar.activation(out=c2v[:, :, :, 0], in_=rpv[:, :, :, 0], func=ACT.Copy, scale=1.0)
            nc.scalar.activation(out=c2v[:, :, :, 1], in_=rpv[:, :, :, 0], func=ACT.Copy, scale=1.0)
            nc.scalar.activation(out=snv[:, :, :, 0], in_=rpv[:, :, :, 1], func=ACT.Copy, scale=1.0)
            nc.scalar.activation(out=snv[:, :, :, 1], in_=rpv[:, :, :, 1], func=ACT.Copy, scale=-1.0)

        def bias_turn():
            bt_ps = prep_ps.tile([P, P], BF16, tag="ps")
            nc.tensor.transpose(bt_ps[:], brow[:], identb[:])
            nc.scalar.copy(out=bias_col[:], in_=bt_ps[:, 0:16])

        xcodes = const.tile([P, PASSES, 1024], U32, tag="xcodes", align_bytes=64)
        xscales = const.tile([P, PASSES, 1024], U8, tag="xscales", align_bytes=64)
        wcodes = const.tile([P, PASSES, 2048], U32, tag="wcodes", align_bytes=64)
        wscales = const.tile([P, PASSES, 2048], U8, tag="wscales", align_bytes=64)

        xg = {}
        wg = {}
        wbf = {}

        def x_prep(k):
            th, sb = k // 2, k % 2
            if sb == 0:
                xg_t = grpp.tile([P, PASSES, 2048], BF16, tag="grp", align_bytes=64)
                xg[th] = xg_t
            words = xraw[k][:].rearrange("p b k -> p (b k)").bitcast(F32)
            xgw = xg[th][:].bitcast(F32)
            for g in range(PASSES):
                xt = prep_ps.tile([P, 2, 256], F32, tag="ps")
                for b in range(2):
                    for u in range(2):
                        lo = b * KW + 256 * g
                        nc.tensor.transpose(xt[:, u, b * P:(b + 1) * P], words[:, lo + u:lo + 256:2], ident[:])
                nc.scalar.copy(out=xgw[:, g, sb * 512:(sb + 1) * 512].rearrange("p (r u) -> p r u", u=2),
                               in_=xt[:].rearrange("p u r -> p r u"))

        def x_quant(th):
            for g in range(PASSES):
                cols = slice(th * 512, (th + 1) * 512)
                nc.vector.quantize_mx(out=xcodes[:, g, cols].bitcast(FP8X4), scales=xscales[:, g, cols], in_=xg[th][:, g, :])

        def w_widen(jj, j2):
            wbf_t = rawp.tile([P, 2, K], BF16, tag="raw")
            wbf[(jj, j2)] = wbf_t
            for a in range(2):
                pieces = PASSES if (jj, j2, a) == (ORDER[0], 0, 0) else 2
                w = K // pieces
                for c in range(pieces):
                    nc.vector.tensor_tensor(out=wbf_t[:, a, c * w:(c + 1) * w], in0=wb[(jj, j2)][:, a, c * w:(c + 1) * w].bitcast(FP8),
                                            in1=sc[:, c * w:(c + 1) * w], op=ALU.mult)

        def w_turn(jj, j2, gs):
            if jj not in wg:
                wg_t = grpp.tile([P, PASSES, 2048], BF16, tag="grp", align_bytes=64)
                wg[jj] = wg_t
            words = wbf[(jj, j2)][:].rearrange("p a k -> p (a k)").bitcast(F32)
            wgw = wg[jj][:].bitcast(F32)
            for g in gs:
                wt = prep_ps.tile([P, 2, 256], F32, tag="ps")
                for a in range(2):
                    for u in range(2):
                        lo = a * KW + 256 * g
                        nc.tensor.transpose(wt[:, u, :].rearrange("p (x a f) -> p x a f", x=2, a=2)[:, :, a, :], words[:, lo + u:lo + 256:2], ident[:])
                nc.scalar.copy(out=wgw[:, g, :].rearrange("p (x j c u) -> p x j c u", x=2, j=2, u=2)[:, :, j2],
                               in_=wt[:].rearrange("p u (x c) -> p x c u", x=2))

        def w_quant(jj, gs):
            for g in gs:
                cols = slice(jj * 512, (jj + 1) * 512)
                nc.vector.quantize_mx(out=wcodes[:, g, cols].bitcast(FP8X4), scales=wscales[:, g, cols], in_=wg[jj][:, g, :])

        ms = {}
        ot = {}

        def mx(jj, th, x):
            tcols = slice(th * 512, (th + 1) * 512)
            for j2 in range(2):
                acc = acc_ps.tile([P, 512], F32, tag="ps")
                c0 = jj * 512 + x * 256 + j2 * P
                for g in range(PASSES):
                    nc.tensor.matmul_mx(out=acc[:],
                                        lhsT=wcodes[:, g, c0:c0 + P].bitcast(FP8X4), lhsT_scale=wscales[:, g, c0:c0 + P],
                                        rhs=xcodes[:, g, tcols].bitcast(FP8X4), rhs_scale=xscales[:, g, tcols],
                                        start=(g == 0), stop=(g == PASSES - 1))
                if x == 0:
                    ms_t = msrp.tile([P, 512], F32, tag="msr")
                else:
                    ms_t = mspp.tile([P, 512], F32, tag="msp")
                ms[(jj, th, x, j2)] = ms_t
                bc = x * 8 + 2 * jj + j2
                nc.scalar.activation(out=ms_t[:], in_=acc[:], func=ACT.Identity, bias=bias_col[:, bc:bc + 1], scale=1.0)

        halves = {}

        def get_ot(jj, k):
            if (jj, k) not in ot:
                ot_t = otp.tile([P, 8, P], F32, tag="ot")
                ot[(jj, k)] = ot_t
                halves[(jj, k)] = 0
            return ot[(jj, k)]

        def half_done(jj, k):
            halves[(jj, k)] = halves[(jj, k)] + 1
            if halves[(jj, k)] == 2:
                o = ot[(jj, k)]
                rows = slice(k * P, (k + 1) * P)
                if jj < 3:
                    nc.sync.dma_start(out=out_0[rows, :, 4 * jj:4 * jj + 4, :], in_=o[:].rearrange("p (b h) f -> p b h f", b=2))
                else:
                    nc.sync.dma_start(out=out_1[rows, :, :, :], in_=o[:, 0:4, :].rearrange("p (b h) f -> p b h f", b=2))
                    nc.sync.dma_start(out=out_2[rows, :, :, :], in_=o[:, 4:8, :].rearrange("p (b h) f -> p b h f", b=2))

        late_bias = []

        def last_tile(jj, k):
            c0 = jj * 512 + 256
            ot_t = get_ot(jj, k)
            bv = bfull[:].rearrange("p (h x f) -> p h x f", x=2, f=64)[:, 4 * jj:4 * jj + 4, 1, :]
            for b in range(2):
                acc = acc_ps.tile([P, 256], F32, tag="ps")
                t0 = (k * 2 + b) * P
                for g in range(PASSES):
                    nc.tensor.matmul_mx(out=acc[:],
                                        lhsT=xcodes[:, g, t0:t0 + P].bitcast(FP8X4), lhsT_scale=xscales[:, g, t0:t0 + P],
                                        rhs=wcodes[:, g, c0:c0 + 256].bitcast(FP8X4), rhs_scale=wscales[:, g, c0:c0 + 256],
                                        start=(g == 0), stop=(g == PASSES - 1))
                nc.vector.tensor_tensor(out=ot_t[:, 4 * b:4 * b + 4, 64:128], in0=acc[:].rearrange("p (h f) -> p h f", f=64), in1=bv, op=ALU.add)
                nc.sync.dma_start(out=out_0[k * P:(k + 1) * P, b, 4 * jj:4 * jj + 4, :], in_=ot_t[:, 4 * b:4 * b + 4, :])

        def mx_tokens(jj, th):
            c0 = jj * 512 + 256
            for sb in range(2):
                k = 2 * th + sb
                if (jj, k) == (ORDER[3], 3):
                    last_tile(jj, k)
                    continue
                acc = acc_ps.tile([P, 2, 256], F32, tag="ps")
                for b in range(2):
                    t0 = (k * 2 + b) * P
                    for g in range(PASSES):
                        nc.tensor.matmul_mx(out=acc[:, b, :],
                                            lhsT=xcodes[:, g, t0:t0 + P].bitcast(FP8X4), lhsT_scale=xscales[:, g, t0:t0 + P],
                                            rhs=wcodes[:, g, c0:c0 + 256].bitcast(FP8X4), rhs_scale=wscales[:, g, c0:c0 + 256],
                                            start=(g == 0), stop=(g == PASSES - 1))
                ot_t = get_ot(jj, k)
                bv = bfull[:].rearrange("p (h x f) -> p h x f", x=2, f=64)[:, 4 * jj:4 * jj + 4, 1, :]
                ov = ot_t[:, :, 64:128].rearrange("p (b h) f -> p b h f", b=2)
                if jj == ORDER[1]:
                    nc.scalar.copy(out=ov, in_=acc[:].rearrange("p b (h f) -> p b h f", f=64))
                    late_bias.append((jj, k, ov, bv))
                else:
                    nc.vector.tensor_tensor(out=ov, in0=acc[:].rearrange("p b (h f) -> p b h f", f=64),
                                            in1=bv.unsqueeze(1).to_broadcast([P, 2, 4, 64]), op=ALU.add)
                    half_done(jj, k)

        late = []
        fence = const.tile([P, 2], BF16, tag="fence")

        def late_adds():
            while len(late) > 0:
                jj, k, ox, qd = late.pop(0)
                nc.gpsimd.tensor_tensor(out=ox.rearrange("p r (i e) -> p r i e", e=2), in0=ox.rearrange("p r (i e) -> p r i e", e=2),
                                        in1=qd[:].rearrange("p r (i e) -> p r i e", e=2)[:, :, :, ::-1], op=ALU.add)
                half_done(jj, k)
            while len(late_bias) > 0:
                jj, k, ov, bv = late_bias.pop(0)
                nc.gpsimd.tensor_tensor(out=ov, in0=ov, in1=bv.unsqueeze(1).to_broadcast([P, 2, 4, 64]), op=ALU.add)
                half_done(jj, k)

        def back(jj, th, x):
            rot = 0
            if x == 0:
                rot = 8 if jj < 3 else 4
            bkv = []
            oxs = []
            for sb in range(2):
                k = 2 * th + sb
                get_ot(jj, k)
                bk = back_ps.tile([P, 4, P], F32, tag="ps")
                for b in range(2):
                    for j2 in range(2):
                        slot = b * 2 + j2 if jj < 3 else j2 * 2 + b
                        t0 = (sb * 2 + b) * P
                        nc.tensor.transpose(bk[:, slot, :], ms[(jj, th, x, j2)][:, t0:t0 + P], ident[:])
                bkv.append(bk[:].rearrange("p s (a f) -> p (s a) f", a=2))
                oxs.append(ot[(jj, k)][:, :, x * 64:(x + 1) * 64])
            pqs = []
            if jj == ORDER[1]:
                for sb in range(2):
                    k = 2 * th + sb
                    qd = qdp.tile([P, 8, 64], F32, tag="qd")
                    nc.vector.tensor_tensor(out=oxs[sb], in0=bkv[sb], in1=tab[:, k, 0, :].unsqueeze(1).to_broadcast([P, 8, 64]), op=ALU.mult)
                    nc.vector.tensor_tensor(out=qd[:], in0=bkv[sb], in1=tab[:, k, 1, :].unsqueeze(1).to_broadcast([P, 8, 64]), op=ALU.mult)
                    late.append((jj, k, oxs[sb], qd))
                return
            if rot > 0:
                for sb in range(2):
                    k = 2 * th + sb
                    pq = pqp.tile([P, 2, 8, 64], F32, tag="pq")
                    pqs.append(pq)
                    nc.vector.tensor_tensor(out=pq[:, :, 0:rot, :],
                                            in0=bkv[sb][:, 0:rot, :].unsqueeze(1).to_broadcast([P, 2, rot, 64]),
                                            in1=tab[:, k, :, :].unsqueeze(2).to_broadcast([P, 2, rot, 64]), op=ALU.mult)
            for sb in range(2):
                k = 2 * th + sb
                if rot < 8:
                    nc.scalar.copy(out=oxs[sb][:, rot:8, :], in_=bkv[sb][:, rot:8, :])
                if rot > 0:
                    eng = nc.vector if jj in ORDER[:2] else nc.gpsimd
                    eng.tensor_tensor(out=oxs[sb][:, 0:rot, :].rearrange("p r (i e) -> p r i e", e=2),
                                            in0=pqs[sb][:, 0, 0:rot, :].rearrange("p r (i e) -> p r i e", e=2),
                                            in1=pqs[sb][:, 1, 0:rot, :].rearrange("p r (i e) -> p r i e", e=2)[:, :, :, ::-1],
                                            op=ALU.add)
                half_done(jj, k)

        allg = [0, 1, 2]
        first = ORDER[0]
        warm(3)
        scales_spread()
        warm(2)
        w_widen(first, 0)
        w_widen(first, 1)
        x_prep(0)
        warm(2)
        x_prep(1)
        warm(2)
        w_turn(first, 0, allg)
        warm(2)
        x_quant(0)
        tables()
        x_prep(2)
        warm(2)
        w_turn(first, 1, allg)
        bias_turn()
        warm(2)
        w_quant(first, allg)
        x_prep(3)
        x_quant(1)
        w_widen(ORDER[1], 0)
        w_widen(ORDER[1], 1)

        subs = [(jj, th, x) for jj in ORDER[:3] for th in range(2) for x in range(2)]
        subs = subs + [(ORDER[3], th, x) for x in range(2) for th in range(2)]
        for n in range(len(subs)):
            if subs[n][0] < 3 and subs[n][2] == 1:
                mx_tokens(subs[n][0], subs[n][1])
            else:
                mx(*subs[n])
            if n > 0 and (subs[n - 1][0] == 3 or subs[n - 1][2] == 0):
                back(*subs[n - 1])
            if n == 2:
                nc.sync.dma_start(out=bfull[:], in_=b_qkv.partition_broadcast(P))
            m = n // 4 + 1
            i = n % 4
            if m < 4 and i < 3:
                w_turn(ORDER[m], 0, [i])
                w_turn(ORDER[m], 1, [i])
                w_quant(ORDER[m], [i])
            if m + 1 < 4 and i in (1, 2):
                w_widen(ORDER[m + 1], i - 1)
            if n == 6:
                nc.gpsimd.tensor_copy(out=fence[:], in_=wbf[(ORDER[3], 1)][:, 1, K - 2:K])
            if n in (6, 7):
                late_adds()
